import numpy as np
import ml_dtypes


def mxq(x, axis, fmt="e4m3"):
    dtype, down = {"e4m3": (ml_dtypes.float8_e4m3fn, 7), "e5m2": (ml_dtypes.float8_e5m2, 14)}[fmt]
    v = np.moveaxis(np.asarray(x, np.float32).astype(ml_dtypes.bfloat16).astype(np.float64), axis, -1)
    blocks = v.reshape(v.shape[:-1] + (-1, 32))
    amax = np.abs(blocks).max(-1, keepdims=True)
    byte = np.maximum(np.where(amax > 0, np.frexp(amax)[1] - 1 + 127, 0) - down, 1)
    scale = np.exp2(byte - 127.0)
    codes = (blocks / scale).astype(np.float32).astype(dtype).astype(np.float64)
    return np.moveaxis((codes * scale).reshape(v.shape), -1, axis)


WIDE = False


def mx_kscale(k):
    if not WIDE:
        return np.ones(k)
    levels = np.array([10, -10, 5, -5, 0])
    if k % 512:
        return np.exp2(np.random.permutation(np.resize(levels, k // 32))).repeat(32)
    a = np.empty((k // 512, 16))
    for p in range(k // 512):
        a[p, :8] = np.random.permutation(np.resize(levels, 8))
        for g in range(8):
            far = levels[np.abs(levels - a[p, g]) >= 10]
            a[p, g + 8] = far[np.random.randint(len(far))]
    return np.exp2(a.ravel()).repeat(32)


BF16 = ml_dtypes.bfloat16


def bf(x):
    return np.asarray(x, np.float32).astype(BF16)


def f64(x):
    return np.asarray(x).astype(np.float64)


E2M1 = np.array([0.0, 0.5, 1.0, 1.5, 2.0, 3.0, 4.0, 6.0, -0.0, -0.5, -1.0, -1.5, -2.0, -3.0, -4.0, -6.0])


def pack_weight(w, fmt):
    k, n = w.shape
    w = f64(bf(w)).reshape(k // 32, 32, n)
    amax = np.abs(w).max(1)
    if fmt == "e4m3":
        byte = np.frexp(amax)[1] - 1 + 127 - 7
    else:
        mant, ex = np.frexp(amax / 6.0)
        byte = np.where(mant > 0.5, ex, ex - 1) + 127
    byte = np.clip(np.where(amax > 0, byte, 1), 1, 254)
    scaled = (w * np.exp2(127.0 - byte)[:, None, :]).reshape(k, n).astype(np.float32)
    by_word = np.ascontiguousarray(scaled.reshape(k // 512, 128, 4, n).transpose(0, 1, 3, 2))
    if fmt == "e4m3":
        words = by_word.astype(ml_dtypes.float8_e4m3fn).view(np.uint8)
    else:
        c = by_word.astype(ml_dtypes.float4_e2m1fn).view(np.uint8) & 0xF
        words = c[..., 0::2] | (c[..., 1::2] << 4)
    return np.ascontiguousarray(words), np.ascontiguousarray(byte.astype(np.uint8).reshape(k // 512, 16, n))


def unpack_weight(words, scales, fmt):
    g, p, n, _ = words.shape
    if fmt == "e4m3":
        vals = np.ascontiguousarray(words).view(ml_dtypes.float8_e4m3fn).astype(np.float64)
    else:
        nib = np.empty((g, p, n, 4), np.uint8)
        nib[..., 0::2] = words & 0xF
        nib[..., 1::2] = words >> 4
        vals = E2M1[nib]
    vals = vals * np.repeat(np.exp2(scales.astype(np.float64) - 127.0), 8, axis=1)[..., None]
    return vals.transpose(0, 1, 3, 2).reshape(g * 512, n)
def pack4(w):
    words, scales = pack_weight(w, "e2m1")
    return words.reshape(words.shape[0], 128, -1), scales


def unpack4(words, scales):
    return unpack_weight(words.reshape(words.shape[0], 128, -1, 2), scales, "e2m1")


B, L, E, QH, KVH, D, FFN = 2, 256, 1024, 8, 2, 128, 4096
KV = KVH * D
EPS = 1.1920928955078125e-07


def rmsnorm(x, w):
    return x / np.sqrt(np.mean(x * x, axis=-1, keepdims=True) + EPS) * w


def draw0():
    s, t = mx_kscale(FFN), mx_kscale(E)
    ffn_act = bf(np.random.standard_normal((B, L, FFN)) * 0.6 * s)
    wd_words, wd_scales = pack4(np.random.standard_normal((FFN, E)) / np.sqrt(FFN) / s[:, None])
    residual = bf(np.random.standard_normal((B, L, E)) * 1.1)
    ln1_w = bf((1.0 + 0.1 * np.random.standard_normal(E)) * t)
    wk_words, wk_scales = pack4(np.random.standard_normal((E, KV)) / np.sqrt(E) / t[:, None])
    wv_words, wv_scales = pack4(np.random.standard_normal((E, KV)) / np.sqrt(E) / t[:, None])
    return {"ffn_act": ffn_act,
            "wd_words": wd_words,
            "wd_scales": wd_scales,
            "residual": residual,
            "ln1_w": ln1_w,
            "wk_words": wk_words,
            "wk_scales": wk_scales,
            "wv_words": wv_words,
            "wv_scales": wv_scales}


def core(ffn_act, wd_words, wd_scales, residual, ln1_w, wk_words, wk_scales, wv_words, wv_scales):
    x_out = (mxq(f64(ffn_act), 2, "e4m3") @ unpack4(wd_words, wd_scales)) + f64(residual)
    hq = mxq(rmsnorm(x_out, f64(ln1_w)), 2, "e4m3")
    k_out = (hq @ unpack4(wk_words, wk_scales)).reshape(B, L, KV)
    v_out = (hq @ unpack4(wv_words, wv_scales)).reshape(B, L, KV)
    return x_out, k_out, v_out


def e4m3fn_bytes(y):
    return np.clip(np.asarray(y, np.float64), -448.0, 448.0).astype(np.float32).astype(ml_dtypes.float8_e4m3fn).view(np.uint8)


def e4m3fn_values(b):
    return np.asarray(b, np.uint8).view(ml_dtypes.float8_e4m3fn).astype(np.float64)


def setup_inputs():
    d = draw0()
    x0 = np.asarray(d['ffn_act']).astype(np.float64)
    s = (np.max(np.abs(x0), axis=(0, 1), keepdims=True) / 448.0).astype(np.float32)
    out = {}
    for k, v in d.items():
        if k == 'ffn_act':
            out['ffn_act_bytes'] = e4m3fn_bytes(x0 / s.astype(np.float64))
            out['ffn_act_scale'] = s
        else:
            out[k] = v
    return out


def reference(ffn_act_bytes, ffn_act_scale, wd_words, wd_scales, residual, ln1_w, wk_words, wk_scales, wv_words, wv_scales):
    return core(e4m3fn_values(ffn_act_bytes) * ffn_act_scale.astype(np.float64), wd_words, wd_scales, residual, ln1_w, wk_words, wk_scales, wv_words, wv_scales)

@@ -1,0 +1,294 @@
+from contextlib import ExitStack
+
+import concourse.mybir as mybir
+from concourse.masks import make_identity
+
+F32 = mybir.dt.float32
+BF16 = mybir.dt.bfloat16
+I32 = mybir.dt.int32
+U32 = mybir.dt.uint32
+U8 = mybir.dt.uint8
+FP8 = mybir.dt.float8_e4m3fn
+FP8X4 = mybir.dt.float8_e4m3fn_x4
+FP4X4 = mybir.dt.float4_e2m1fn_x4
+ALU = mybir.AluOpType
+ACT = mybir.ActivationFunctionType
+
+P = 128
+TOK, K1, E, KV = 512, 4096, 1024, 256
+EPS = 2.0**-23
+FLOPS = 2 * TOK * K1 * E + 2 * TOK * E * 2 * KV
+
+UNITS = [((0, g), (1, g)) for g in range(8)] + [
+    ((t, 2 * n), (t, 2 * n + 1)) for t in (2, 3) for n in range(4)
+]
+ORDER = """
+M0 M1 R0 E0 M2 R1 Q0 M3 R2 E1 m0 M4 Q1 E2 m1 M5 Q2 R3 M6 R4 E3 R5 M7 m2 Q3 E4 M8 m3 E5 M9 R6 Q4 M10 R7 E6 R8
+M11 R9 Q5 E7 m4 M12 Q6 m5 E8 m6 Q7 E9 m7 Q8 Q9 R10 A00 R11 A01 S00 R12 E10 S01 B0 M13 A10 A11 M14 R13 E11 m8
+S10 E12 S11 B1 R14 q0 M15 Q10 m9 c0 E13 q1 R15 Q11 E14 m10 N00 m11 c1 Q12 Q13 m12 N01 N10 H0 E15 m13 h0 Q14
+Q15 A20 m14 A21 S20 N11 m15 S21 B2 Z0 A30 q2 H1 c2 A31 S30 N20 S31 B3 N21 q3 h1 c3 H2 N30 K0 h2 N31 k0 Z1 H3
+Z2 K1 h3 K2 k1 Z3 K3 k2 k3
+""".split()
+
+
+def tile_textencoderblock_pc_w4_kernel(
+    tc, act, act_scale, wd_words, wd_scales, residual, ln1_w,
+    wk_words, wk_scales, wv_words, wv_scales, x_out, k_out, v_out,
+):
+    nc = tc.nc
+    with ExitStack() as ctx:
+        keep = ctx.enter_context(tc.tile_pool(name="keep", bufs=1))
+        work = ctx.enter_context(tc.tile_pool(name="work", bufs=2))
+        psum = ctx.enter_context(tc.psum_pool(name="psum", bufs=4))
+
+        ident = keep.tile([P, P], F32, name="ident")
+        make_identity(nc, ident[:])
+        ctx.enter_context(tc.manual_schedule())
+
+        act_rows = act.rearrange("b l k -> (b l) k")
+        x_rows = x_out.rearrange("b l e -> (b l) e")
+        k_rows = k_out.rearrange("b l c -> (b l) c")
+        v_rows = v_out.rearrange("b l c -> (b l) c")
+        res_rows = residual.rearrange("b l e -> (b l) e")
+
+        warm = keep.tile([P, 1], F32, name="warm")
+        nc.vector.memset(warm[:], 1.0)
+        wd_sc = keep.tile([P, 8, E], U8, name="wd_sc", align_bytes=64)
+        nc.vector.memset(wd_sc[:, 0:2, :].bitcast(I32), 0)
+        nc.vector.memset(wd_sc[:, 2:8, :].bitcast(I32), 0)
+        wkv_sc = keep.tile([P, 2, 2 * KV], U8, name="wkv_sc", align_bytes=64)
+        nc.vector.memset(wkv_sc[:].bitcast(I32), 0)
+
+        sc = keep.tile([P, 8, 8], F32, name="sc")
+        nc.scalar.dma_start(
+            out=sc[:, :, 0:4],
+            in_=act_scale.rearrange("a o (g p t) -> p (a o g) t", p=P, t=4),
+        )
+        warm2 = keep.tile([P, 1], F32, name="warm2")
+        nc.scalar.activation(warm2[:], warm[:], ACT.Sqrt)
+
+        act01 = act_rows[0:256].rearrange("(j p) k -> p j k", p=P)
+        pair = []
+        cuts = [(0, 512), (512, 1024), (1024, 2048), (2048, 3072), (3072, 4096)]
+        for n, (lo, hi) in enumerate(cuts):
+            pair.append(keep.tile([P, 2, hi - lo], U8, name=f"pair{n}"))
+
+        def load_pair(n):
+            lo, hi = cuts[n]
+            nc.sync.dma_start(out=pair[n][:], in_=act01[:, :, lo:hi])
+
+        wd = [keep.tile([P, 2, 2 * E], U8, name=f"wd{n}", align_bytes=64) for n in range(4)]
+
+        def load_wd(n):
+            nc.sync.dma_start(out=wd[n][:], in_=wd_words[2 * n : 2 * n + 2].rearrange("g p n -> p g n"))
+
+        def load_wd_scales(lo, hi):
+            for q in range(4):
+                nc.sync.dma_start(
+                    out=wd_sc[32 * q : 32 * q + 4, lo:hi, :].bitcast(I32),
+                    in_=wd_scales[lo:hi, 4 * q : 4 * q + 4, :].rearrange("g q n -> q g n").bitcast(I32),
+                )
+
+        single = [keep.tile([P, K1], U8, name=f"single{t}") for t in (2, 3)]
+        res = [keep.tile([P, 2, E], BF16, name=f"res{n}") for n in range(2)]
+
+        def load_res(n):
+            nc.sync.dma_start(out=res[n][:], in_=res_rows[256 * n : 256 * n + 256].rearrange("(j p) e -> p j e", p=P))
+
+        load_pair(0)
+        load_pair(1)
+        load_wd_scales(0, 2)
+        load_wd(0)
+        load_pair(2)
+        load_wd_scales(2, 8)
+        load_wd(1)
+        load_pair(3)
+        load_wd(2)
+        load_pair(4)
+        load_wd(3)
+        nc.sync.dma_start(out=single[0][:], in_=act_rows[256:384])
+        load_res(0)
+        nc.sync.dma_start(out=single[1][:], in_=act_rows[384:512])
+        lnw = keep.tile([P, E], BF16, name="lnw")
+        nc.sync.dma_start(out=lnw[:], in_=ln1_w.partition_broadcast(P))
+        wkv = keep.tile([P, 2, 4 * KV], U8, name="wkv", align_bytes=64)
+        for n, words in enumerate((wk_words, wv_words)):
+            nc.sync.dma_start(out=wkv[:, :, 512 * n : 512 * n + 512], in_=words.rearrange("g p n -> p g n"))
+        for n, scales in enumerate((wk_scales, wv_scales)):
+            for q in range(4):
+                nc.sync.dma_start(
+                    out=wkv_sc[32 * q : 32 * q + 4, :, KV * n : KV * n + KV].bitcast(I32),
+                    in_=scales[:, 4 * q : 4 * q + 4, :].rearrange("g q n -> q g n").bitcast(I32),
+                )
+        load_res(1)
+
+        wide, turned, grouped, codes, scales_of = {}, {}, {}, {}, {}
+        acc, xs, stats, small, h_rows, h_turned, h_grouped, h_codes, kv_acc = {}, {}, {}, {}, {}, {}, {}, {}, {}
+
+        def bytes_of(tile, g, width):
+            k = 512 * g
+            if tile < 2:
+                for n, (lo, hi) in enumerate(cuts):
+                    if lo <= k < hi:
+                        return pair[n][:, tile, k - lo : k - lo + width]
+            return single[tile - 2][:, k : k + width]
+
+        def cast(i):
+            (t0, g0), (t1, g1) = UNITS[i]
+            w = work.tile([P, 2, 512], BF16, name="wide", bufs=16)
+            wide[i] = w
+            if t0 == t1:
+                nc.scalar.copy(w[:].rearrange("p j k -> p (j k)"), bytes_of(t0, g0, 1024).bitcast(FP8))
+            else:
+                nc.scalar.copy(w[:, 0, :], bytes_of(t0, g0, 512).bitcast(FP8))
+                nc.scalar.copy(w[:, 1, :], bytes_of(t1, g1, 512).bitcast(FP8))
+
+        def turn(i):
+            bank = psum.tile([P, 2, 2, P], F32, name="bank")
+            turned[i] = bank
+            for j in range(2):
+                words = wide[i][:, j, :].bitcast(F32)
+                for u in range(2):
+                    nc.tensor.transpose(bank[:, u, j, :], words[:, u:256:2], ident[:])
+
+        def scale(i):
+            (t0, g0), (t1, g1) = UNITS[i]
+            grp = work.tile([P, 256, 4], BF16, name="grp", bufs=4, align_bytes=64)
+            grouped[i] = grp
+            vals = turned[i][:].bitcast(BF16)
+            if g0 == g1:
+                nc.vector.tensor_tensor(
+                    out=grp[:].rearrange("p r (u e) -> p r u e", u=2),
+                    in0=vals.rearrange("p u j (r e) -> p (j r) u e", e=2),
+                    in1=sc[:, g0, 0:4].rearrange("p (u e) -> p u e", u=2).unsqueeze(1).to_broadcast([P, 256, 2, 2]),
+                    op=ALU.mult,
+                )
+            else:
+                for j, g in enumerate((g0, g1)):
+                    nc.vector.tensor_tensor(
+                        out=grp[:, P * j : P * j + P, :].rearrange("p r (u e) -> p r u e", u=2),
+                        in0=vals[:, :, j, :].rearrange("p u (r e) -> p r u e", e=2),
+                        in1=sc[:, g, 0:4].rearrange("p (u e) -> p u e", u=2).unsqueeze(1).to_broadcast([P, P, 2, 2]),
+                        op=ALU.mult,
+                    )
+
+        def quant(i):
+            c = work.tile([P, 256], U32, name="codes", bufs=16, align_bytes=64)
+            s = work.tile([P, 256], U8, name="cscales", bufs=16, align_bytes=64)
+            codes[i], scales_of[i] = c, s
+            nc.vector.quantize_mx(out=c[:].bitcast(FP8X4), scales=s[:], in_=grouped[i][:].rearrange("p r t -> p (r t)"))
+
+        def product(i, j, half):
+            tile, g = UNITS[i][j]
+            if (tile, half) not in acc:
+                a = psum.tile([P, 512], F32, name="acc")
+                acc[(tile, half)] = a
+            nc.tensor.matmul_mx(
+                out=acc[(tile, half)][:],
+                lhsT=codes[i][:, P * j : P * j + P].bitcast(FP8X4),
+                lhsT_scale=scales_of[i][:, P * j : P * j + P],
+                rhs=wd[g // 2][:, g % 2, E * half : E * half + E].bitcast(FP4X4),
+                rhs_scale=wd_sc[:, g, 512 * half : 512 * half + 512],
+                start=(g == 0),
+                stop=(g == 7),
+            )
+
+        def multiply(i):
+            if i >= 14:
+                for n in (14, 15):
+                    for j in range(2):
+                        product(n, j, i - 14)
+            else:
+                for j in range(2):
+                    for half in range(2):
+                        product(i, j, half)
+
+        def add(t, half):
+            if half == 0:
+                x = keep.tile([P, E], F32, name=f"x{t}")
+                st = keep.tile([P, 2], F32, name=f"st{t}")
+                xs[t], stats[t] = x, st
+            cols = slice(512 * half, 512 * half + 512)
+            nc.vector.tensor_tensor(out=xs[t][:, cols], in0=acc[(t, half)][:], in1=res[t // 2][:, t % 2, cols], op=ALU.add)
+            nc.sync.dma_start(out=x_rows[P * t : P * t + P, cols], in_=xs[t][:, cols])
+
+        def square(t, half):
+            cols = slice(512 * half, 512 * half + 512)
+            junk = work.tile([P, 512], BF16, name="junk", bufs=2)
+            nc.scalar.activation(junk[:], xs[t][:, cols], ACT.Square, accum_out=stats[t][:, half : half + 1])
+
+        def bias(t):
+            b = keep.tile([P, 1], F32, name=f"b{t}")
+            small[t] = b
+            nc.gpsimd.tensor_scalar(out=b[:], in0=stats[t][:, 0:1], scalar1=1.0 / E, scalar2=EPS, op0=ALU.mult, op1=ALU.add)
+
+        def root(t):
+            r = keep.tile([P, 1], F32, name=f"r{t}")
+            nc.scalar.activation(r[:], stats[t][:, 1:2], ACT.Sqrt, bias=small[t][:], scale=1.0 / E)
+            small[t] = r
+
+        def invert(t):
+            r = keep.tile([P, 1], F32, name=f"rstd{t}")
+            nc.vector.reciprocal(r[:], small[t][:])
+            small[t] = r
+
+        def norm(t, u):
+            if u == 0:
+                h = work.tile([P, 2, 512], BF16, name="h", bufs=4)
+                h_rows[t] = h
+            nc.vector.scalar_tensor_tensor(
+                out=h_rows[t][:, u, :].rearrange("p (w e) -> p w e", e=2),
+                in0=xs[t][:].rearrange("p (w u e) -> p u w e", u=2, e=2)[:, u],
+                scalar=small[t][:],
+                in1=lnw[:].rearrange("p (w u e) -> p u w e", u=2, e=2)[:, u],
+                op0=ALU.mult,
+                op1=ALU.mult,
+            )
+
+        def turn_h(t):
+            bank = psum.tile([P, 2, 2, P], F32, name="bank")
+            h_turned[t] = bank
+            for g in range(2):
+                for u in range(2):
+                    nc.tensor.transpose(bank[:, u, g, :], h_rows[t][:, u, 256 * g : 256 * g + 256].bitcast(F32), ident[:])
+
+        def group_h(t):
+            hg = work.tile([P, 256, 4], BF16, name="hg", bufs=2, align_bytes=64)
+            h_grouped[t] = hg
+            nc.scalar.copy(hg[:].bitcast(F32), h_turned[t][:].rearrange("p u g r -> p (g r) u"))
+
+        def quant_h(t):
+            c = work.tile([P, 256], U32, name="hcodes", bufs=2, align_bytes=64)
+            s = work.tile([P, 256], U8, name="hscales", bufs=2, align_bytes=64)
+            h_codes[t] = (c, s)
+            nc.vector.quantize_mx(out=c[:].bitcast(FP8X4), scales=s[:], in_=h_grouped[t][:].rearrange("p r t -> p (r t)"))
+
+        def project(t):
+            a = psum.tile([P, 2, 2, P], F32, name="bank")
+            kv_acc[t] = a
+            c, s = h_codes[t]
+            for g in range(2):
+                nc.tensor.matmul_mx(
+                    out=a[:].rearrange("p a b c -> p (a b c)"),
+                    lhsT=c[:, P * g : P * g + P].bitcast(FP8X4),
+                    lhsT_scale=s[:, P * g : P * g + P],
+                    rhs=wkv[:, g, :].bitcast(FP4X4),
+                    rhs_scale=wkv_sc[:, g, :],
+                    start=(g == 0),
+                    stop=(g == 1),
+                )
+
+        def emit_kv(t):
+            kv = work.tile([P, 512], F32, name="kv", bufs=4)
+            nc.scalar.copy(kv[:], kv_acc[t][:].rearrange("p a b c -> p (a b c)"))
+            nc.sync.dma_start(out=k_rows[P * t : P * t + P], in_=kv[:, 0:KV])
+            nc.sync.dma_start(out=v_rows[P * t : P * t + P], in_=kv[:, KV : 2 * KV])
+
+        steps = {"M": cast, "R": turn, "E": scale, "Q": quant, "m": multiply, "A": add, "S": square, "B": bias,
+                 "q": root, "c": invert, "N": norm, "H": turn_h, "h": group_h, "Z": quant_h, "K": project, "k": emit_kv}
+        for step in ORDER:
+            kind, what = step[0:1], step[1:]
+            if kind in ("A", "S", "N"):
+                steps[kind](int(what[0:1]), int(what[1:2]))
+            else:
+                steps[kind](int(what))

@@ -23,11 +23,11 @@ UNITS = [((0, g), (1, g)) for g in range(8)] + [
     ((t, 2 * n), (t, 2 * n + 1)) for t in (2, 3) for n in range(4)
 ]
 ORDER = """
-M0 M1 R0 E0 M2 R1 Q0 M3 R2 E1 m0 M4 Q1 E2 m1 M5 Q2 R3 M6 R4 E3 R5 M7 m2 Q3 E4 M8 m3 E5 M9 R6 Q4 M10 R7 E6 R8
-M11 R9 Q5 E7 m4 M12 Q6 m5 E8 m6 Q7 E9 m7 Q8 Q9 R10 A00 R11 A01 S00 R12 E10 S01 B0 M13 A10 A11 M14 R13 E11 m8
-S10 E12 S11 B1 R14 q0 M15 Q10 m9 c0 E13 q1 R15 Q11 E14 m10 N00 m11 c1 Q12 Q13 m12 N01 N10 H0 E15 m13 h0 Q14
-Q15 A20 m14 A21 S20 N11 m15 S21 B2 Z0 A30 q2 H1 c2 A31 S30 N20 S31 B3 N21 q3 h1 c3 H2 N30 K0 h2 N31 k0 Z1 H3
-Z2 K1 h3 K2 k1 Z3 K3 k2 k3
+D0 D1 M0a M1 M0b D2 R0a R0b E0a D3 R1 E0b D4 M2 E1 D5 D6 D7 M3 Q0 R2 m0 E2 M4 Q1 R3 M5 R4 E3 M6 m1 Q2 Q3 M7 R5
+E4 R6 M8 m2 Q4 E5 M9 m3 E6 M10 R7 Q5 M11 R8 E7 m4 M12 Q6 E8 R9 M13 R10 E9 m5 Q7 Q8 m6 E10 m7 Q9 Q10 R11 A00
+R12 A01 S00 E11 m8 S01 B0 q0 A10 M14 R13 Q11 c0 E12 m9 S10 M15 B1 N00 m10 Q12 N01 m11 E13 R14 A11 R15 Q13 S11
+E14 m12 q1 c1 E15 H0 m13 Q14 Q15 A20 m14 A21 S20 N10 m15 S21 B2 A30 h0 N11 q2 S30 Z0 H1 c2 A31 B3 K0 h1 N20
+S31 N21 q3 Z1 k0 H2 c3 N30 K1 h2 N31 H30 k1 Z2 H31 h30 K2 h31 Z30 K30 Z31 k2 K31 k3
 """.split()
 
 
@@ -51,6 +51,8 @@ def tile_textencoderblock_pc_w4_kernel(
         v_rows = v_out.rearrange("b l c -> (b l) c")
         res_rows = residual.rearrange("b l e -> (b l) e")
 
+        zeros = keep.tile([P, 512], BF16, name="zeros")
+        nc.vector.memset(zeros[:], 0.0)
         warm = keep.tile([P, 1], F32, name="warm")
         nc.vector.memset(warm[:], 1.0)
         wd_sc = keep.tile([P, 8, E], U8, name="wd_sc", align_bytes=64)
@@ -60,10 +62,9 @@ def tile_textencoderblock_pc_w4_kernel(
         nc.vector.memset(wkv_sc[:].bitcast(I32), 0)
 
         sc = keep.tile([P, 8, 8], F32, name="sc")
-        nc.scalar.dma_start(
-            out=sc[:, :, 0:4],
-            in_=act_scale.rearrange("a o (g p t) -> p (a o g) t", p=P, t=4),
-        )
+        sc_view = act_scale.rearrange("a o (g p t) -> p (a o g) t", p=P, t=4)
+        for lo, hi in ((0, 2), (2, 8)):
+            nc.scalar.dma_start(out=sc[:, lo:hi, 0:4], in_=sc_view[:, lo:hi, :])
         warm2 = keep.tile([P, 1], F32, name="warm2")
         nc.scalar.activation(warm2[:], warm[:], ACT.Sqrt)
 
@@ -97,9 +98,9 @@ def tile_textencoderblock_pc_w4_kernel(
 
         load_pair(0)
         load_pair(1)
+        load_pair(2)
         load_wd_scales(0, 2)
         load_wd(0)
-        load_pair(2)
         load_wd_scales(2, 8)
         load_wd(1)
         load_pair(3)
@@ -143,20 +144,36 @@ def tile_textencoderblock_pc_w4_kernel(
                 nc.scalar.copy(w[:, 0, :], bytes_of(t0, g0, 512).bitcast(FP8))
                 nc.scalar.copy(w[:, 1, :], bytes_of(t1, g1, 512).bitcast(FP8))
 
-        def turn(i):
-            bank = psum.tile([P, 2, 2, P], F32, name="bank")
-            turned[i] = bank
-            for j in range(2):
+        def cast_first(j):
+            if j == 0:
+                w = work.tile([P, 2, 512], BF16, name="wide", bufs=16)
+                wide[0] = w
+            nc.vector.tensor_copy(wide[0][:, j, :], bytes_of(j, 0, 512).bitcast(FP8))
+
+        def keep_warm(n):
+            if n == 0:
+                d = psum.tile([P, 512], F32, name="acc")
+                small["dummy"] = d
+            nc.tensor.matmul(small["dummy"][:], lhsT=zeros[:, 0:P], rhs=zeros[:], start=True, stop=True)
+
+        def turn(i, only=(0, 1)):
+            if only[0] == 0:
+                bank = psum.tile([P, 2, 2, P], F32, name="bank")
+                turned[i] = bank
+            bank = turned[i]
+            for j in only:
                 words = wide[i][:, j, :].bitcast(F32)
                 for u in range(2):
                     nc.tensor.transpose(bank[:, u, j, :], words[:, u:256:2], ident[:])
 
-        def scale(i):
+        def scale(i, only=(0, 1)):
             (t0, g0), (t1, g1) = UNITS[i]
-            grp = work.tile([P, 256, 4], BF16, name="grp", bufs=4, align_bytes=64)
-            grouped[i] = grp
+            if only[0] == 0:
+                grp = work.tile([P, 256, 4], BF16, name="grp", bufs=4, align_bytes=64)
+                grouped[i] = grp
+            grp = grouped[i]
             vals = turned[i][:].bitcast(BF16)
-            if g0 == g1:
+            if g0 == g1 and len(only) == 2:
                 nc.vector.tensor_tensor(
                     out=grp[:].rearrange("p r (u e) -> p r u e", u=2),
                     in0=vals.rearrange("p u j (r e) -> p (j r) u e", e=2),
@@ -164,7 +181,8 @@ def tile_textencoderblock_pc_w4_kernel(
                     op=ALU.mult,
                 )
             else:
-                for j, g in enumerate((g0, g1)):
+                for j in only:
+                    g = (g0, g1)[j]
                     nc.vector.tensor_tensor(
                         out=grp[:, P * j : P * j + P, :].rearrange("p r (u e) -> p r u e", u=2),
                         in0=vals[:, :, j, :].rearrange("p u (r e) -> p r u e", e=2),
@@ -236,6 +254,13 @@ def tile_textencoderblock_pc_w4_kernel(
             if u == 0:
                 h = work.tile([P, 2, 512], BF16, name="h", bufs=4)
                 h_rows[t] = h
+            if t == 3:
+                cols = slice(512 * u, 512 * u + 512)
+                nc.vector.scalar_tensor_tensor(
+                    out=h_rows[t][:, u, :], in0=xs[t][:, cols], scalar=small[t][:], in1=lnw[:, cols],
+                    op0=ALU.mult, op1=ALU.mult,
+                )
+                return
             nc.vector.scalar_tensor_tensor(
                 out=h_rows[t][:, u, :].rearrange("p (w e) -> p w e", e=2),
                 in0=xs[t][:].rearrange("p (w u e) -> p u w e", u=2, e=2)[:, u],
@@ -252,6 +277,33 @@ def tile_textencoderblock_pc_w4_kernel(
                 for u in range(2):
                     nc.tensor.transpose(bank[:, u, g, :], h_rows[t][:, u, 256 * g : 256 * g + 256].bitcast(F32), ident[:])
 
+        def turn_h_last(g):
+            if g == 0:
+                bank = psum.tile([P, 2, 2, P], F32, name="bank")
+                h_turned[3] = bank
+            words = h_rows[3][:, g, :].bitcast(F32)
+            for u in range(2):
+                nc.tensor.transpose(h_turned[3][:, u, g, :], words[:, u:256:2], ident[:])
+
+        def group_h_last(g):
+            if g == 0:
+                hg = work.tile([P, 256, 4], BF16, name="hg", bufs=2, align_bytes=64)
+                h_grouped[3] = hg
+            nc.scalar.copy(
+                h_grouped[3][:, P * g : P * g + P, :].bitcast(F32), h_turned[3][:, :, g, :].rearrange("p u r -> p r u")
+            )
+
+        def quant_h_last(g):
+            if g == 0:
+                c = work.tile([P, 256], U32, name="hcodes", bufs=2, align_bytes=64)
+                s = work.tile([P, 256], U8, name="hscales", bufs=2, align_bytes=64)
+                h_codes[3] = (c, s)
+            c, s = h_codes[3]
+            cols = slice(P * g, P * g + P)
+            nc.vector.quantize_mx(
+                out=c[:, cols].bitcast(FP8X4), scales=s[:, cols], in_=h_grouped[3][:, cols, :].rearrange("p r t -> p (r t)")
+            )
+
         def group_h(t):
             hg = work.tile([P, 256, 4], BF16, name="hg", bufs=2, align_bytes=64)
             h_grouped[t] = hg
@@ -263,11 +315,13 @@ def tile_textencoderblock_pc_w4_kernel(
             h_codes[t] = (c, s)
             nc.vector.quantize_mx(out=c[:].bitcast(FP8X4), scales=s[:], in_=h_grouped[t][:].rearrange("p r t -> p (r t)"))
 
-        def project(t):
-            a = psum.tile([P, 2, 2, P], F32, name="bank")
-            kv_acc[t] = a
+        def project(t, only=(0, 1)):
+            if only[0] == 0:
+                a = psum.tile([P, 2, 2, P], F32, name="bank")
+                kv_acc[t] = a
+            a = kv_acc[t]
             c, s = h_codes[t]
-            for g in range(2):
+            for g in only:
                 nc.tensor.matmul_mx(
                     out=a[:].rearrange("p a b c -> p (a b c)"),
                     lhsT=c[:, P * g : P * g + P].bitcast(FP8X4),
@@ -282,7 +336,8 @@ def tile_textencoderblock_pc_w4_kernel(
             kv = work.tile([P, 512], F32, name="kv", bufs=4)
             nc.scalar.copy(kv[:], kv_acc[t][:].rearrange("p a b c -> p (a b c)"))
             nc.sync.dma_start(out=k_rows[P * t : P * t + P], in_=kv[:, 0:KV])
-            nc.sync.dma_start(out=v_rows[P * t : P * t + P], in_=kv[:, KV : 2 * KV])
+            v_queue = nc.scalar if t == 3 else nc.sync
+            v_queue.dma_start(out=v_rows[P * t : P * t + P], in_=kv[:, KV : 2 * KV])
 
         steps = {"M": cast, "R": turn, "E": scale, "Q": quant, "m": multiply, "A": add, "S": square, "B": bias,
                  "q": root, "c": invert, "N": norm, "H": turn_h, "h": group_h, "Z": quant_h, "K": project, "k": emit_kv}
@@ -290,5 +345,25 @@ def tile_textencoderblock_pc_w4_kernel(
             kind, what = step[0:1], step[1:]
             if kind in ("A", "S", "N"):
                 steps[kind](int(what[0:1]), int(what[1:2]))
+            elif kind == "D":
+                keep_warm(int(what))
+            elif what == "0a" or what == "0b":
+                j = 0 if what == "0a" else 1
+                if kind == "M":
+                    cast_first(j)
+                elif kind == "R":
+                    turn(0, (j,))
+                else:
+                    scale(0, (j,))
+            elif kind in ("H", "h", "Z", "K") and len(what) == 2:
+                g = int(what[1:2])
+                if kind == "H":
+                    turn_h_last(g)
+                elif kind == "h":
+                    group_h_last(g)
+                elif kind == "Z":
+                    quant_h_last(g)
+                else:
+                    project(3, (g,))
             else:
                 steps[kind](int(what))

@@ -23,11 +23,11 @@ UNITS = [((0, g), (1, g)) for g in range(8)] + [
     ((t, 2 * n), (t, 2 * n + 1)) for t in (2, 3) for n in range(4)
 ]
 ORDER = """
-D0 D1 M0a M1 M0b D2 R0a R0b E0a D3 R1 E0b D4 M2 E1 D5 D6 D7 M3 Q0 R2 m0 E2 M4 Q1 R3 M5 R4 E3 M6 m1 Q2 Q3 M7 R5
-E4 R6 M8 m2 Q4 E5 M9 m3 E6 M10 R7 Q5 M11 R8 E7 m4 M12 Q6 E8 R9 M13 R10 E9 m5 Q7 Q8 m6 E10 m7 Q9 Q10 R11 A00
-R12 A01 S00 E11 m8 S01 B0 q0 A10 M14 R13 Q11 c0 E12 m9 S10 M15 B1 N00 m10 Q12 N01 m11 E13 R14 A11 R15 Q13 S11
-E14 m12 q1 c1 E15 H0 m13 Q14 Q15 A20 m14 A21 S20 N10 m15 S21 B2 A30 h0 N11 q2 S30 Z0 H1 c2 A31 B3 K0 h1 N20
-S31 N21 q3 Z1 k0 H2 c3 N30 K1 h2 N31 H30 k1 Z2 H31 h30 K2 h31 Z30 K30 Z31 k2 K31 k3
+D0 D1 M0a M1 M0b D2 X0 R0a M2 R0b C0 D3 E0a R1 E0b M3 D4 D5 Q0 R2 E1 m0 M4 Q1 E2 M5 R3 m1 E3 M6 R4 Q2 M7 R5 E4
+m2 M8 Q3 Q4 M9 R6 E5 m3 M10 E6 R7 M11 Q5 R8 E7 m4 M12 E8 M13 R9 R10 Q6 Q7 m5 Q8 E9 m6 E10 m7 Q9 Q10 R11 A00
+R12 A01 S00 E11 m8 M14 B0 E12 S01 R13 m9 q0 Q11 M15 A10 c0 E13 S10 R14 R15 B1 Q12 m10 A11 N00 S11 m11 Q13 N01
+E14 H0 m12 h0 E15 q1 m13 Q14 Q15 c1 A20 m14 A21 S20 N10 m15 S21 B2 A30 N11 S30 A31 H1 q2 B3 c2 Z0 S31 N20 K0
+h1 N21 q3 c3 Z1 H2 N30 k0 K1 N31 h2 H30 H31 Z2 h30 K2 h31 Z30 k1 K30 Z31 k2 K31 k3
 """.split()
 
 
@@ -51,6 +51,8 @@ def tile_textencoderblock_pc_w4_kernel(
         v_rows = v_out.rearrange("b l c -> (b l) c")
         res_rows = residual.rearrange("b l e -> (b l) e")
 
+        s_rows = keep.tile([P, 512], F32, name="s_rows")
+        nc.vector.memset(s_rows[:], 0.0)
         zeros = keep.tile([P, 512], BF16, name="zeros")
         nc.vector.memset(zeros[:], 0.0)
         warm = keep.tile([P, 1], F32, name="warm")
@@ -61,10 +63,8 @@ def tile_textencoderblock_pc_w4_kernel(
         wkv_sc = keep.tile([P, 2, 2 * KV], U8, name="wkv_sc", align_bytes=64)
         nc.vector.memset(wkv_sc[:].bitcast(I32), 0)
 
-        sc = keep.tile([P, 8, 8], F32, name="sc")
-        sc_view = act_scale.rearrange("a o (g p t) -> p (a o g) t", p=P, t=4)
-        for lo, hi in ((0, 2), (2, 8)):
-            nc.scalar.dma_start(out=sc[:, lo:hi, 0:4], in_=sc_view[:, lo:hi, :])
+        sc = keep.tile([P, 8, 4], F32, name="sc")
+        nc.scalar.dma_start(out=s_rows[0:8, :], in_=act_scale.rearrange("a o (g c) -> (a o g) c", g=8))
         warm2 = keep.tile([P, 1], F32, name="warm2")
         nc.scalar.activation(warm2[:], warm[:], ACT.Sqrt)
 
@@ -155,6 +155,15 @@ def tile_textencoderblock_pc_w4_kernel(
                 d = psum.tile([P, 512], F32, name="acc")
                 small["dummy"] = d
             nc.tensor.matmul(small["dummy"][:], lhsT=zeros[:, 0:P], rhs=zeros[:], start=True, stop=True)
+
+        def turn_scales(n):
+            bank = psum.tile([P, 4, P], F32, name="acc")
+            small["scales"] = bank
+            for t in range(4):
+                nc.tensor.transpose(bank[:, t, :], s_rows[:, t:512:4], ident[:])
+
+        def keep_scales(n):
+            nc.vector.tensor_copy(sc[:], small["scales"][:, :, 0:8].rearrange("p t g -> p g t"))
 
         def turn(i, only=(0, 1)):
             if only[0] == 0:
@@ -339,7 +348,7 @@ def tile_textencoderblock_pc_w4_kernel(
             v_queue = nc.scalar if t == 3 else nc.sync
             v_queue.dma_start(out=v_rows[P * t : P * t + P], in_=kv[:, KV : 2 * KV])
 
-        steps = {"M": cast, "R": turn, "E": scale, "Q": quant, "m": multiply, "A": add, "S": square, "B": bias,
+        steps = {"X": turn_scales, "C": keep_scales, "M": cast, "R": turn, "E": scale, "Q": quant, "m": multiply, "A": add, "S": square, "B": bias,
                  "q": root, "c": invert, "N": norm, "H": turn_h, "h": group_h, "Z": quant_h, "K": project, "k": emit_kv}
         for step in ORDER:
             kind, what = step[0:1], step[1:]

@@ -23,11 +23,12 @@ UNITS = [((0, g), (1, g)) for g in range(8)] + [
     ((t, 2 * n), (t, 2 * n + 1)) for t in (2, 3) for n in range(4)
 ]
 ORDER = """
-D0 D1 M0a M1 M0b D2 X0 R0a M2 R0b C0 D3 E0a R1 E0b M3 D4 D5 Q0 R2 E1 m0 M4 Q1 E2 M5 R3 m1 E3 M6 R4 Q2 M7 R5 E4
-m2 M8 Q3 Q4 M9 R6 E5 m3 M10 E6 R7 M11 Q5 R8 E7 m4 M12 E8 M13 R9 R10 Q6 Q7 m5 Q8 E9 m6 E10 m7 Q9 Q10 R11 A00
-R12 A01 S00 E11 m8 M14 B0 E12 S01 R13 m9 q0 Q11 M15 A10 c0 E13 S10 R14 R15 B1 Q12 m10 A11 N00 S11 m11 Q13 N01
-E14 H0 m12 h0 E15 q1 m13 Q14 Q15 c1 A20 m14 A21 S20 N10 m15 S21 B2 A30 N11 S30 A31 H1 q2 B3 c2 Z0 S31 N20 K0
-h1 N21 q3 c3 Z1 H2 N30 k0 K1 N31 h2 H30 H31 Z2 h30 K2 h31 Z30 k1 K30 Z31 k2 K31 k3
+Dstart Dstart M0a Dstart X0 M0b M1 R0a R0b C0 Dstart M2 E0a R1 E0b Dstart M3 R2 Q0 E1 Dstart m0 Q1 M4 R3 E2 m1
+M5 Q2 E3 DR4 M6 R4 R5 E4 M7 m2 Q3 Q4 M8 R6 E5 m3 M9 Q5 E6 R7 M10 R8 E7 DR9 M11 m4 Q6 M12 E8 DR9 R9 R10 M13 Q7
+Q8 m5 E9 M14 m6 E10 M15 m7 Q9 Q10 R11 A00 R12 A01 DR13 S00 DR13 E11 R13 S01 B0 R14 q0 E12 DR15 m8 c0 A10 m9
+Q11 S10 N00 N01 m10 B1 E13 DR15 R15 Q12 Q13 H0 A11 DH1 m11 E14 S11 m12 q1 E15 m13 Q14 Q15 c1 A20 m14 A21 S20
+N10 m15 S21 B2 A30 q2 N11 h0 DH1 A31 S30 H1 c2 Z0 S31 N20 B3 K0 h1 N21 q3 k0 H2 c3 Z1 DK1 N30 K1 h2 N31 H30 Z2
+H31 h30 K2 h31 Z30 k1 Z31 K30 k2 K31 k3
 """.split()
 
 
@@ -101,11 +102,11 @@ def tile_textencoderblock_pc_w4_kernel(
         load_pair(2)
         load_wd_scales(0, 2)
         load_wd(0)
+        load_pair(3)
         load_wd_scales(2, 8)
         load_wd(1)
-        load_pair(3)
-        load_wd(2)
         load_pair(4)
+        load_wd(2)
         load_wd(3)
         nc.sync.dma_start(out=single[0][:], in_=act_rows[256:384])
         load_res(0)
@@ -150,11 +151,18 @@ def tile_textencoderblock_pc_w4_kernel(
                 wide[0] = w
             nc.vector.tensor_copy(wide[0][:, j, :], bytes_of(j, 0, 512).bitcast(FP8))
 
-        def keep_warm(n):
-            if n == 0:
-                d = psum.tile([P, 512], F32, name="acc")
-                small["dummy"] = d
-            nc.tensor.matmul(small["dummy"][:], lhsT=zeros[:, 0:P], rhs=zeros[:], start=True, stop=True)
+        banks = {}
+
+        def bank_of(user):
+            if user not in banks:
+                bank = psum.tile([P, 2, 2, P], F32, name="acc" if user == "start" else "bank")
+                banks[user] = bank
+            return banks[user]
+
+        def keep_warm(user):
+            nc.tensor.matmul(
+                bank_of(user)[:].rearrange("p a b c -> p (a b c)"), lhsT=zeros[:, 0:P], rhs=zeros[:], start=True, stop=True
+            )
 
         def turn_scales(n):
             bank = psum.tile([P, 4, P], F32, name="acc")
@@ -166,10 +174,8 @@ def tile_textencoderblock_pc_w4_kernel(
             nc.vector.tensor_copy(sc[:], small["scales"][:, :, 0:8].rearrange("p t g -> p g t"))
 
         def turn(i, only=(0, 1)):
-            if only[0] == 0:
-                bank = psum.tile([P, 2, 2, P], F32, name="bank")
-                turned[i] = bank
-            bank = turned[i]
+            bank = bank_of(f"R{i}")
+            turned[i] = bank
             for j in only:
                 words = wide[i][:, j, :].bitcast(F32)
                 for u in range(2):
@@ -280,16 +286,14 @@ def tile_textencoderblock_pc_w4_kernel(
             )
 
         def turn_h(t):
-            bank = psum.tile([P, 2, 2, P], F32, name="bank")
+            bank = bank_of(f"H{t}")
             h_turned[t] = bank
             for g in range(2):
                 for u in range(2):
                     nc.tensor.transpose(bank[:, u, g, :], h_rows[t][:, u, 256 * g : 256 * g + 256].bitcast(F32), ident[:])
 
         def turn_h_last(g):
-            if g == 0:
-                bank = psum.tile([P, 2, 2, P], F32, name="bank")
-                h_turned[3] = bank
+            h_turned[3] = bank_of("H3")
             words = h_rows[3][:, g, :].bitcast(F32)
             for u in range(2):
                 nc.tensor.transpose(h_turned[3][:, u, g, :], words[:, u:256:2], ident[:])
@@ -325,10 +329,8 @@ def tile_textencoderblock_pc_w4_kernel(
             nc.vector.quantize_mx(out=c[:].bitcast(FP8X4), scales=s[:], in_=h_grouped[t][:].rearrange("p r t -> p (r t)"))
 
         def project(t, only=(0, 1)):
-            if only[0] == 0:
-                a = psum.tile([P, 2, 2, P], F32, name="bank")
-                kv_acc[t] = a
-            a = kv_acc[t]
+            a = bank_of(f"K{t}")
+            kv_acc[t] = a
             c, s = h_codes[t]
             for g in only:
                 nc.tensor.matmul_mx(
@@ -355,7 +357,7 @@ def tile_textencoderblock_pc_w4_kernel(
             if kind in ("A", "S", "N"):
                 steps[kind](int(what[0:1]), int(what[1:2]))
             elif kind == "D":
-                keep_warm(int(what))
+                keep_warm(what)
             elif what == "0a" or what == "0b":
                 j = 0 if what == "0a" else 1
                 if kind == "M":

from contextlib import ExitStack

import concourse.mybir as mybir
from concourse.masks import make_identity

F32 = mybir.dt.float32
BF16 = mybir.dt.bfloat16
I32 = mybir.dt.int32
U32 = mybir.dt.uint32
U8 = mybir.dt.uint8
FP8 = mybir.dt.float8_e4m3fn
FP8X4 = mybir.dt.float8_e4m3fn_x4
FP4X4 = mybir.dt.float4_e2m1fn_x4
ALU = mybir.AluOpType
ACT = mybir.ActivationFunctionType

P = 128
TOK, K1, E, KV = 512, 4096, 1024, 256
EPS = 2.0**-23
FLOPS = 2 * TOK * K1 * E + 2 * TOK * E * 2 * KV

UNITS = [((0, g), (1, g)) for g in range(8)] + [
    ((t, 2 * n), (t, 2 * n + 1)) for t in (2, 3) for n in range(4)
]
ORDER = """
Dstart Dstart M0a Dstart X0 M0b M1 R0a R0b C0 Dstart M2 E0a R1 E0b Dstart M3 R2 Q0 E1 Dstart m0 Q1 M4 R3 E2 m1
M5 Q2 E3 DR4 M6 R4 R5 E4 M7 m2 Q3 Q4 M8 R6 E5 m3 M9 Q5 E6 R7 M10 R8 E7 DR9 M11 m4 Q6 M12 E8 DR9 R9 R10 M13 Q7
Q8 m5 E9 M14 m6 E10 M15 m7 Q9 Q10 R11 A00 R12 A01 DR13 S00 DR13 E11 R13 S01 B0 R14 q0 E12 DR15 m8 c0 A10 m9
Q11 S10 N00 N01 m10 B1 E13 DR15 R15 Q12 Q13 H0 A11 DH1 m11 E14 S11 m12 q1 E15 m13 Q14 Q15 c1 A20 m14 A21 S20
N10 m15 S21 B2 A30 q2 N11 h0 DH1 A31 S30 H1 c2 Z0 S31 N20 B3 K0 h1 N21 q3 k0 H2 c3 Z1 DK1 N30 K1 h2 N31 H30 Z2
H31 h30 K2 h31 Z30 k1 Z31 K30 k2 K31 k3
""".split()


def tile_textencoderblock_pc_w4_kernel(
    tc, act, act_scale, wd_words, wd_scales, residual, ln1_w,
    wk_words, wk_scales, wv_words, wv_scales, x_out, k_out, v_out,
):
    nc = tc.nc
    with ExitStack() as ctx:
        keep = ctx.enter_context(tc.tile_pool(name="keep", bufs=1))
        work = ctx.enter_context(tc.tile_pool(name="work", bufs=2))
        psum = ctx.enter_context(tc.psum_pool(name="psum", bufs=4))

        ident = keep.tile([P, P], F32, name="ident")
        make_identity(nc, ident[:])
        ctx.enter_context(tc.manual_schedule())

        act_rows = act.rearrange("b l k -> (b l) k")
        x_rows = x_out.rearrange("b l e -> (b l) e")
        k_rows = k_out.rearrange("b l c -> (b l) c")
        v_rows = v_out.rearrange("b l c -> (b l) c")
        res_rows = residual.rearrange("b l e -> (b l) e")

        s_rows = keep.tile([P, 512], F32, name="s_rows")
        nc.vector.memset(s_rows[:], 0.0)
        zeros = keep.tile([P, 512], BF16, name="zeros")
        nc.vector.memset(zeros[:], 0.0)
        warm = keep.tile([P, 1], F32, name="warm")
        nc.vector.memset(warm[:], 1.0)
        wd_sc = keep.tile([P, 8, E], U8, name="wd_sc", align_bytes=64)
        nc.vector.memset(wd_sc[:, 0:2, :].bitcast(I32), 0)
        nc.vector.memset(wd_sc[:, 2:8, :].bitcast(I32), 0)
        wkv_sc = keep.tile([P, 2, 2 * KV], U8, name="wkv_sc", align_bytes=64)
        nc.vector.memset(wkv_sc[:].bitcast(I32), 0)

        sc = keep.tile([P, 8, 4], F32, name="sc")
        nc.scalar.dma_start(out=s_rows[0:8, :], in_=act_scale.rearrange("a o (g c) -> (a o g) c", g=8))
        warm2 = keep.tile([P, 1], F32, name="warm2")
        nc.scalar.activation(warm2[:], warm[:], ACT.Sqrt)

        act01 = act_rows[0:256].rearrange("(j p) k -> p j k", p=P)
        pair = []
        cuts = [(0, 512), (512, 1024), (1024, 2048), (2048, 3072), (3072, 4096)]
        for n, (lo, hi) in enumerate(cuts):
            pair.append(keep.tile([P, 2, hi - lo], U8, name=f"pair{n}"))

        def load_pair(n):
            lo, hi = cuts[n]
            nc.sync.dma_start(out=pair[n][:], in_=act01[:, :, lo:hi])

        wd = [keep.tile([P, 2, 2 * E], U8, name=f"wd{n}", align_bytes=64) for n in range(4)]

        def load_wd(n):
            nc.sync.dma_start(out=wd[n][:], in_=wd_words[2 * n : 2 * n + 2].rearrange("g p n -> p g n"))

        def load_wd_scales(lo, hi):
            for q in range(4):
                nc.sync.dma_start(
                    out=wd_sc[32 * q : 32 * q + 4, lo:hi, :].bitcast(I32),
                    in_=wd_scales[lo:hi, 4 * q : 4 * q + 4, :].rearrange("g q n -> q g n").bitcast(I32),
                )

        single = [keep.tile([P, K1], U8, name=f"single{t}") for t in (2, 3)]
        res = [keep.tile([P, 2, E], BF16, name=f"res{n}") for n in range(2)]

        def load_res(n):
            nc.sync.dma_start(out=res[n][:], in_=res_rows[256 * n : 256 * n + 256].rearrange("(j p) e -> p j e", p=P))

        load_pair(0)
        load_pair(1)
        load_pair(2)
        load_wd_scales(0, 2)
        load_wd(0)
        load_pair(3)
        load_wd_scales(2, 8)
        load_wd(1)
        load_pair(4)
        load_wd(2)
        load_wd(3)
        nc.sync.dma_start(out=single[0][:], in_=act_rows[256:384])
        load_res(0)
        nc.sync.dma_start(out=single[1][:], in_=act_rows[384:512])
        lnw = keep.tile([P, E], BF16, name="lnw")
        nc.sync.dma_start(out=lnw[:], in_=ln1_w.partition_broadcast(P))
        wkv = keep.tile([P, 2, 4 * KV], U8, name="wkv", align_bytes=64)
        for n, words in enumerate((wk_words, wv_words)):
            nc.sync.dma_start(out=wkv[:, :, 512 * n : 512 * n + 512], in_=words.rearrange("g p n -> p g n"))
        for n, scales in enumerate((wk_scales, wv_scales)):
            for q in range(4):
                nc.sync.dma_start(
                    out=wkv_sc[32 * q : 32 * q + 4, :, KV * n : KV * n + KV].bitcast(I32),
                    in_=scales[:, 4 * q : 4 * q + 4, :].rearrange("g q n -> q g n").bitcast(I32),
                )
        load_res(1)

        wide, turned, grouped, codes, scales_of = {}, {}, {}, {}, {}
        acc, xs, stats, small, h_rows, h_turned, h_grouped, h_codes, kv_acc = {}, {}, {}, {}, {}, {}, {}, {}, {}

        def bytes_of(tile, g, width):
            k = 512 * g
            if tile < 2:
                for n, (lo, hi) in enumerate(cuts):
                    if lo <= k < hi:
                        return pair[n][:, tile, k - lo : k - lo + width]
            return single[tile - 2][:, k : k + width]

        def cast(i):
            (t0, g0), (t1, g1) = UNITS[i]
            w = work.tile([P, 2, 512], BF16, name="wide", bufs=16)
            wide[i] = w
            if t0 == t1:
                nc.scalar.copy(w[:].rearrange("p j k -> p (j k)"), bytes_of(t0, g0, 1024).bitcast(FP8))
            else:
                nc.scalar.copy(w[:, 0, :], bytes_of(t0, g0, 512).bitcast(FP8))
                nc.scalar.copy(w[:, 1, :], bytes_of(t1, g1, 512).bitcast(FP8))

        def cast_first(j):
            if j == 0:
                w = work.tile([P, 2, 512], BF16, name="wide", bufs=16)
                wide[0] = w
            nc.vector.tensor_copy(wide[0][:, j, :], bytes_of(j, 0, 512).bitcast(FP8))

        banks = {}

        def bank_of(user):
            if user not in banks:
                bank = psum.tile([P, 2, 2, P], F32, name="acc" if user == "start" else "bank")
                banks[user] = bank
            return banks[user]

        def keep_warm(user):
            nc.tensor.matmul(
                bank_of(user)[:].rearrange("p a b c -> p (a b c)"), lhsT=zeros[:, 0:P], rhs=zeros[:], start=True, stop=True
            )

        def turn_scales(n):
            bank = psum.tile([P, 4, P], F32, name="acc")
            small["scales"] = bank
            for t in range(4):
                nc.tensor.transpose(bank[:, t, :], s_rows[:, t:512:4], ident[:])

        def keep_scales(n):
            nc.vector.tensor_copy(sc[:], small["scales"][:, :, 0:8].rearrange("p t g -> p g t"))

        def turn(i, only=(0, 1)):
            bank = bank_of(f"R{i}")
            turned[i] = bank
            for j in only:
                words = wide[i][:, j, :].bitcast(F32)
                for u in range(2):
                    nc.tensor.transpose(bank[:, u, j, :], words[:, u:256:2], ident[:])

        def scale(i, only=(0, 1)):
            (t0, g0), (t1, g1) = UNITS[i]
            if only[0] == 0:
                grp = work.tile([P, 256, 4], BF16, name="grp", bufs=4, align_bytes=64)
                grouped[i] = grp
            grp = grouped[i]
            vals = turned[i][:].bitcast(BF16)
            if g0 == g1 and len(only) == 2:
                nc.vector.tensor_tensor(
                    out=grp[:].rearrange("p r (u e) -> p r u e", u=2),
                    in0=vals.rearrange("p u j (r e) -> p (j r) u e", e=2),
                    in1=sc[:, g0, 0:4].rearrange("p (u e) -> p u e", u=2).unsqueeze(1).to_broadcast([P, 256, 2, 2]),
                    op=ALU.mult,
                )
            else:
                for j in only:
                    g = (g0, g1)[j]
                    nc.vector.tensor_tensor(
                        out=grp[:, P * j : P * j + P, :].rearrange("p r (u e) -> p r u e", u=2),
                        in0=vals[:, :, j, :].rearrange("p u (r e) -> p r u e", e=2),
                        in1=sc[:, g, 0:4].rearrange("p (u e) -> p u e", u=2).unsqueeze(1).to_broadcast([P, P, 2, 2]),
                        op=ALU.mult,
                    )

        def quant(i):
            c = work.tile([P, 256], U32, name="codes", bufs=16, align_bytes=64)
            s = work.tile([P, 256], U8, name="cscales", bufs=16, align_bytes=64)
            codes[i], scales_of[i] = c, s
            nc.vector.quantize_mx(out=c[:].bitcast(FP8X4), scales=s[:], in_=grouped[i][:].rearrange("p r t -> p (r t)"))

        def product(i, j, half):
            tile, g = UNITS[i][j]
            if (tile, half) not in acc:
                a = psum.tile([P, 512], F32, name="acc")
                acc[(tile, half)] = a
            nc.tensor.matmul_mx(
                out=acc[(tile, half)][:],
                lhsT=codes[i][:, P * j : P * j + P].bitcast(FP8X4),
                lhsT_scale=scales_of[i][:, P * j : P * j + P],
                rhs=wd[g // 2][:, g % 2, E * half : E * half + E].bitcast(FP4X4),
                rhs_scale=wd_sc[:, g, 512 * half : 512 * half + 512],
                start=(g == 0),
                stop=(g == 7),
            )

        def multiply(i):
            if i >= 14:
                for n in (14, 15):
                    for j in range(2):
                        product(n, j, i - 14)
            else:
                for j in range(2):
                    for half in range(2):
                        product(i, j, half)

        def add(t, half):
            if half == 0:
                x = keep.tile([P, E], F32, name=f"x{t}")
                st = keep.tile([P, 2], F32, name=f"st{t}")
                xs[t], stats[t] = x, st
            cols = slice(512 * half, 512 * half + 512)
            nc.vector.tensor_tensor(out=xs[t][:, cols], in0=acc[(t, half)][:], in1=res[t // 2][:, t % 2, cols], op=ALU.add)
            nc.sync.dma_start(out=x_rows[P * t : P * t + P, cols], in_=xs[t][:, cols])

        def square(t, half):
            cols = slice(512 * half, 512 * half + 512)
            junk = work.tile([P, 512], BF16, name="junk", bufs=2)
            nc.scalar.activation(junk[:], xs[t][:, cols], ACT.Square, accum_out=stats[t][:, half : half + 1])

        def bias(t):
            b = keep.tile([P, 1], F32, name=f"b{t}")
            small[t] = b
            nc.gpsimd.tensor_scalar(out=b[:], in0=stats[t][:, 0:1], scalar1=1.0 / E, scalar2=EPS, op0=ALU.mult, op1=ALU.add)

        def root(t):
            r = keep.tile([P, 1], F32, name=f"r{t}")
            nc.scalar.activation(r[:], stats[t][:, 1:2], ACT.Sqrt, bias=small[t][:], scale=1.0 / E)
            small[t] = r

        def invert(t):
            r = keep.tile([P, 1], F32, name=f"rstd{t}")
            nc.vector.reciprocal(r[:], small[t][:])
            small[t] = r

        def norm(t, u):
            if u == 0:
                h = work.tile([P, 2, 512], BF16, name="h", bufs=4)
                h_rows[t] = h
            if t == 3:
                cols = slice(512 * u, 512 * u + 512)
                nc.vector.scalar_tensor_tensor(
                    out=h_rows[t][:, u, :], in0=xs[t][:, cols], scalar=small[t][:], in1=lnw[:, cols],
                    op0=ALU.mult, op1=ALU.mult,
                )
                return
            nc.vector.scalar_tensor_tensor(
                out=h_rows[t][:, u, :].rearrange("p (w e) -> p w e", e=2),
                in0=xs[t][:].rearrange("p (w u e) -> p u w e", u=2, e=2)[:, u],
                scalar=small[t][:],
                in1=lnw[:].rearrange("p (w u e) -> p u w e", u=2, e=2)[:, u],
                op0=ALU.mult,
                op1=ALU.mult,
            )

        def turn_h(t):
            bank = bank_of(f"H{t}")
            h_turned[t] = bank
            for g in range(2):
                for u in range(2):
                    nc.tensor.transpose(bank[:, u, g, :], h_rows[t][:, u, 256 * g : 256 * g + 256].bitcast(F32), ident[:])

        def turn_h_last(g):
            h_turned[3] = bank_of("H3")
            words = h_rows[3][:, g, :].bitcast(F32)
            for u in range(2):
                nc.tensor.transpose(h_turned[3][:, u, g, :], words[:, u:256:2], ident[:])

        def group_h_last(g):
            if g == 0:
                hg = work.tile([P, 256, 4], BF16, name="hg", bufs=2, align_bytes=64)
                h_grouped[3] = hg
            nc.scalar.copy(
                h_grouped[3][:, P * g : P * g + P, :].bitcast(F32), h_turned[3][:, :, g, :].rearrange("p u r -> p r u")
            )

        def quant_h_last(g):
            if g == 0:
                c = work.tile([P, 256], U32, name="hcodes", bufs=2, align_bytes=64)
                s = work.tile([P, 256], U8, name="hscales", bufs=2, align_bytes=64)
                h_codes[3] = (c, s)
            c, s = h_codes[3]
            cols = slice(P * g, P * g + P)
            nc.vector.quantize_mx(
                out=c[:, cols].bitcast(FP8X4), scales=s[:, cols], in_=h_grouped[3][:, cols, :].rearrange("p r t -> p (r t)")
            )

        def group_h(t):
            hg = work.tile([P, 256, 4], BF16, name="hg", bufs=2, align_bytes=64)
            h_grouped[t] = hg
            nc.scalar.copy(hg[:].bitcast(F32), h_turned[t][:].rearrange("p u g r -> p (g r) u"))

        def quant_h(t):
            c = work.tile([P, 256], U32, name="hcodes", bufs=2, align_bytes=64)
            s = work.tile([P, 256], U8, name="hscales", bufs=2, align_bytes=64)
            h_codes[t] = (c, s)
            nc.vector.quantize_mx(out=c[:].bitcast(FP8X4), scales=s[:], in_=h_grouped[t][:].rearrange("p r t -> p (r t)"))

        def project(t, only=(0, 1)):
            a = bank_of(f"K{t}")
            kv_acc[t] = a
            c, s = h_codes[t]
            for g in only:
                nc.tensor.matmul_mx(
                    out=a[:].rearrange("p a b c -> p (a b c)"),
                    lhsT=c[:, P * g : P * g + P].bitcast(FP8X4),
                    lhsT_scale=s[:, P * g : P * g + P],
                    rhs=wkv[:, g, :].bitcast(FP4X4),
                    rhs_scale=wkv_sc[:, g, :],
                    start=(g == 0),
                    stop=(g == 1),
                )

        def emit_kv(t):
            kv = work.tile([P, 512], F32, name="kv", bufs=4)
            nc.scalar.copy(kv[:], kv_acc[t][:].rearrange("p a b c -> p (a b c)"))
            nc.sync.dma_start(out=k_rows[P * t : P * t + P], in_=kv[:, 0:KV])
            v_queue = nc.scalar if t == 3 else nc.sync
            v_queue.dma_start(out=v_rows[P * t : P * t + P], in_=kv[:, KV : 2 * KV])

        steps = {"X": turn_scales, "C": keep_scales, "M": cast, "R": turn, "E": scale, "Q": quant, "m": multiply, "A": add, "S": square, "B": bias,
                 "q": root, "c": invert, "N": norm, "H": turn_h, "h": group_h, "Z": quant_h, "K": project, "k": emit_kv}
        for step in ORDER:
            kind, what = step[0:1], step[1:]
            if kind in ("A", "S", "N"):
                steps[kind](int(what[0:1]), int(what[1:2]))
            elif kind == "D":
                keep_warm(what)
            elif what == "0a" or what == "0b":
                j = 0 if what == "0a" else 1
                if kind == "M":
                    cast_first(j)
                elif kind == "R":
                    turn(0, (j,))
                else:
                    scale(0, (j,))
            elif kind in ("H", "h", "Z", "K") and len(what) == 2:
                g = int(what[1:2])
                if kind == "H":
                    turn_h_last(g)
                elif kind == "h":
                    group_h_last(g)
                elif kind == "Z":
                    quant_h_last(g)
                else:
                    project(3, (g,))
            else:
                steps[kind](int(what))
